import numpy as np
import ml_dtypes


def mxq(x, axis, fmt="e4m3"):
    dtype, down = {"e4m3": (ml_dtypes.float8_e4m3fn, 7), "e5m2": (ml_dtypes.float8_e5m2, 14)}[fmt]
    v = np.moveaxis(np.asarray(x, np.float32).astype(ml_dtypes.bfloat16).astype(np.float64), axis, -1)
    blocks = v.reshape(v.shape[:-1] + (-1, 32))
    amax = np.abs(blocks).max(-1, keepdims=True)
    byte = np.maximum(np.where(amax > 0, np.frexp(amax)[1] - 1 + 127, 0) - down, 1)
    scale = np.exp2(byte - 127.0)
    codes = (blocks / scale).astype(np.float32).astype(dtype).astype(np.float64)
    return np.moveaxis((codes * scale).reshape(v.shape), -1, axis)


WIDE = False


def mx_kscale(k):
    if not WIDE:
        return np.ones(k)
    levels = np.array([10, -10, 5, -5, 0])
    if k % 512:
        return np.exp2(np.random.permutation(np.resize(levels, k // 32))).repeat(32)
    a = np.empty((k // 512, 16))
    for p in range(k // 512):
        a[p, :8] = np.random.permutation(np.resize(levels, 8))
        for g in range(8):
            far = levels[np.abs(levels - a[p, g]) >= 10]
            a[p, g + 8] = far[np.random.randint(len(far))]
    return np.exp2(a.ravel()).repeat(32)


BF16 = ml_dtypes.bfloat16


def bf(x):
    return np.asarray(x, np.float32).astype(BF16)


def f64(x):
    return np.asarray(x).astype(np.float64)


B, S, DIM, HEADS = 1, 4096, 512, 4
HD = DIM // HEADS
EPS = 1e-6


def rms_norm(x, g):
    var = np.mean(np.square(x), axis=-1, keepdims=True)
    return x * (1.0 / np.sqrt(var + EPS)) * g


def rope(x, cos, sin):
    x1, x2 = np.split(x, 2, axis=-1)
    rot = np.concatenate([-x2, x1], axis=-1)
    return x * cos[None, :, None, :] + rot * sin[None, :, None, :]


def setup_inputs():
    s = mx_kscale(DIM)
    return {
        "hidden_states": bf(np.random.standard_normal((B, S, DIM)) * s),
        "cos": bf(np.random.uniform(-1.0, 1.0, (S, HD))),
        "sin": bf(np.random.uniform(-1.0, 1.0, (S, HD))),
        "w_qk": bf(np.random.standard_normal((DIM + DIM, DIM)) / np.sqrt(DIM) / s[None, :]),
        "b_qk": bf(np.random.standard_normal(DIM + DIM) * 0.2),
        "g_q": bf(1.0 + 0.1 * np.random.standard_normal(DIM)),
        "g_k": bf(1.0 + 0.1 * np.random.standard_normal(DIM)),
    }


def reference(hidden_states, cos, sin, w_qk, b_qk, g_q, g_k):
    c, sn = f64(cos), f64(sin)
    qk = (mxq(f64(hidden_states), 2, "e4m3") @ mxq(f64(w_qk), 1, "e4m3").T) + f64(b_qk)
    q = rms_norm(qk[:, :, :DIM], f64(g_q)).reshape(B, S, HEADS, HD)
    k = rms_norm(qk[:, :, DIM:], f64(g_k)).reshape(B, S, HEADS, HD)
    return rope(q, c, sn), rope(k, c, sn)

@@ -1,0 +1,350 @@
+from contextlib import ExitStack
+
+import concourse.mybir as mybir
+from concourse.masks import make_identity
+
+F32 = mybir.dt.float32
+BF16 = mybir.dt.bfloat16
+U32 = mybir.dt.uint32
+U8 = mybir.dt.uint8
+FP8X4 = mybir.dt.float8_e4m3fn_x4
+ACT = mybir.ActivationFunctionType
+ALU = mybir.AluOpType
+
+P = 128
+TOKENS = 4096
+DIM = 512
+HEAD = 128
+HALF = HEAD // 2
+HEADS = DIM // HEAD
+SIDES = 2
+WORDS = DIM // 2
+TILES = TOKENS // P
+GROUP = 4
+GROUPS = TILES // GROUP
+GROUP_TOKENS = GROUP * P
+UNITS = GROUPS * SIDES
+STEPS = 2 * UNITS
+EPS = 1e-6
+
+FLOPS = 2 * TOKENS * SIDES * DIM * DIM
+
+
+def turn_two_blocks(nc, bank, ident, two_blocks):
+    for blk in range(2):
+        for u in range(2):
+            nc.tensor.transpose(bank[:, blk, u, :], two_blocks[:, blk, u:WORDS:2], ident)
+
+
+def copy_two_blocks(nc, bank, grouped, on_scalar):
+    planes = bank[:].rearrange("p b u r -> p b r u")
+    if on_scalar:
+        nc.scalar.copy(out=grouped, in_=planes)
+    else:
+        nc.vector.tensor_copy(out=grouped, in_=planes)
+
+
+def tile_dynamicselfattention_pa_t_kernel(
+    tc, hidden_states, cos, sin, w_qk, b_qk, g_q, g_k, out_0, out_1
+):
+    nc = tc.nc
+    h_dram = hidden_states.flatten_outer_dims().rearrange("(p T) k -> p T k", T=TILES)
+    cos_dram = cos.rearrange("(p T) d -> p T d", T=TILES)
+    sin_dram = sin.rearrange("(p T) d -> p T d", T=TILES)
+    w_dram = w_qk.rearrange("(j p) k -> p j k", p=P)
+    out_dram = [
+        o.flatten_outer_dims().rearrange("(p T h) d -> p T (h d)", T=TILES, h=HEADS)
+        for o in (out_0, out_1)
+    ]
+
+    with ExitStack() as stack:
+        stack.enter_context(tc.manual_schedule())
+        keep = stack.enter_context(tc.tile_pool(name="keep", bufs=1))
+        quant = stack.enter_context(tc.tile_pool(name="quant", bufs=2))
+        zt_pool = stack.enter_context(tc.tile_pool(name="zt_pool", bufs=16))
+        ysq_pool = stack.enter_context(tc.tile_pool(name="ysq_pool", bufs=12))
+        small = stack.enter_context(tc.tile_pool(name="small", bufs=4))
+        cos_pool = stack.enter_context(tc.tile_pool(name="cos_pool", bufs=7))
+        sin_pool = stack.enter_context(tc.tile_pool(name="sin_pool", bufs=6))
+        junk_pool = stack.enter_context(tc.tile_pool(name="junk_pool", bufs=2))
+        bank_pool = stack.enter_context(tc.psum_pool(name="bank_pool", bufs=6))
+        ss_pool = stack.enter_context(tc.psum_pool(name="ss_pool", bufs=2))
+
+        eps = keep.tile([P, 1], F32)
+        nc.vector.memset(eps[:], EPS)
+        warm = keep.tile([P, 1], F32)
+        nc.scalar.activation(out=warm[:], in_=eps[:], func=ACT.Sqrt)
+        vec_rows = keep.tile([P, P], BF16)
+        nc.vector.memset(vec_rows[:], 0.0)
+        ident = keep.tile([P, P], F32)
+        make_identity(nc, ident[:])
+
+        w_sb = keep.tile([P, SIDES * HEADS * DIM], BF16)
+        w_rows = w_sb[:].rearrange("p (j k) -> p j k", k=DIM)
+        h_sb = keep.tile([P, TILES * DIM], BF16)
+        h_rows = h_sb[:].rearrange("p (T k) -> p T k", k=DIM)
+
+        def load_w(pair):
+            two = slice(2 * pair, 2 * pair + 2)
+            nc.sync.dma_start(out=w_rows[:, two, :], in_=w_dram[:, two, :])
+
+        def load_h(g):
+            four = slice(g * GROUP, (g + 1) * GROUP)
+            nc.sync.dma_start(out=h_rows[:, four, :], in_=h_dram[:, four, :])
+
+        nc.scalar.dma_start(out=vec_rows[0:8, :], in_=b_qk.rearrange("(j d) -> j d", d=HEAD))
+        nc.scalar.dma_start(out=vec_rows[8:12, :], in_=g_q.rearrange("(j d) -> j d", d=HEAD))
+        nc.scalar.dma_start(out=vec_rows[12:16, :], in_=g_k.rearrange("(j d) -> j d", d=HEAD))
+        load_w(0)
+        load_h(0)
+        for pair in range(1, SIDES * HEADS // 2):
+            load_w(pair)
+        cos_sb = keep.tile([P, TILES, HEAD], BF16)
+        sin_swap = keep.tile([P, TILES, HEAD], BF16)
+        for part in range(2):
+            for g in range(max(1, part * GROUPS // 2), (part + 1) * GROUPS // 2):
+                load_h(g)
+            some = slice(part * TILES // 2, (part + 1) * TILES // 2)
+            nc.sync.dma_start(out=cos_sb[:, some, :], in_=cos_dram[:, some, :])
+            nc.sync.dma_start(out=sin_swap[:, some, 0:HALF], in_=sin_dram[:, some, HALF:HEAD])
+            nc.sync.dma_start(out=sin_swap[:, some, HALF:HEAD], in_=sin_dram[:, some, 0:HALF])
+
+        w_words = w_sb[:].bitcast(F32).rearrange("p (j w) -> p j w", w=WORDS)
+        h_words = h_sb[:].bitcast(F32).rearrange("p (T w) -> p T w", w=WORDS)
+        w_grouped = keep.tile([P, SIDES * DIM * 4], BF16, align_bytes=64)
+        w_grouped_words = w_grouped[:].bitcast(F32).rearrange("p (j r u) -> p j r u", r=P, u=2)
+        w_codes = keep.tile([P, SIDES * DIM], U32, align_bytes=64)
+        w_scales = keep.tile([P, SIDES * DIM], U8, align_bytes=64)
+        h_codes = keep.tile([P, TOKENS], U32, align_bytes=64)
+        h_scales = keep.tile([P, TOKENS], U8, align_bytes=64)
+        h_grouped = {}
+
+        def turn_weights(pair, on_scalar):
+            bank = bank_pool.tile([P, 2, 2, P], F32, tag="bank")
+            two = slice(2 * pair, 2 * pair + 2)
+            turn_two_blocks(nc, bank, ident[:], w_words[:, two, :])
+            copy_two_blocks(nc, bank, w_grouped_words[:, two], on_scalar)
+
+        def quantise_weights(pair):
+            nc.vector.quantize_mx(
+                out=w_codes[:, 2 * P * pair : 2 * P * (pair + 1)].bitcast(FP8X4),
+                scales=w_scales[:, 2 * P * pair : 2 * P * (pair + 1)],
+                in_=w_grouped[:, 8 * P * pair : 8 * P * (pair + 1)],
+            )
+
+        def turn_hidden(g, second_on_scalar):
+            h_grouped[g] = quant.tile([P, GROUP_TOKENS * 4], BF16, align_bytes=64, name="h_grouped")
+            words = h_grouped[g][:].bitcast(F32).rearrange("p (t r u) -> p t r u", r=P, u=2)
+            for pair in range(GROUP // 2):
+                first = g * GROUP + 2 * pair
+                bank = bank_pool.tile([P, 2, 2, P], F32, tag="bank")
+                turn_two_blocks(nc, bank, ident[:], h_words[:, first : first + 2, :])
+                copy_two_blocks(
+                    nc, bank, words[:, 2 * pair : 2 * pair + 2], second_on_scalar and pair == 1
+                )
+
+        def quantise_hidden(g):
+            tokens = slice(g * GROUP_TOKENS, (g + 1) * GROUP_TOKENS)
+            nc.vector.quantize_mx(
+                out=h_codes[:, tokens].bitcast(FP8X4), scales=h_scales[:, tokens], in_=h_grouped[g][:]
+            )
+
+        vec_f32 = keep.tile([P, P], F32)
+        nc.vector.tensor_copy(out=vec_f32[:], in_=vec_rows[:])
+        vec_ps = bank_pool.tile([P, P], F32, tag="bank")
+        nc.tensor.transpose(vec_ps[:], vec_f32[:], ident[:])
+        cols = keep.tile([P, 16], F32)
+        nc.vector.tensor_copy(out=cols[:], in_=vec_ps[:, 0:16])
+        bias_col = cols[:, 0:8]
+        gain_col = cols[:, 8:16]
+        gain_bias = keep.tile([P, 8], F32)
+        nc.vector.tensor_mul(out=gain_bias[:], in0=bias_col, in1=gain_col)
+
+        turn_weights(0, False)
+        turn_hidden(0, True)
+        quantise_weights(0)
+        for pair in range(1, SIDES * HEADS // 2):
+            turn_weights(pair, True)
+        quantise_hidden(0)
+        for pair in range(1, SIDES * HEADS // 2):
+            quantise_weights(pair)
+
+        acc = {}
+        zt = {}
+        ysq = {}
+        sq = {}
+        ss = {}
+        std = {}
+        rstd = {}
+        z = {}
+        with_cos = {}
+        with_sin = {}
+
+        def project(s):
+            if s < 0 or s >= STEPS:
+                return
+            unit = s // 2
+            tokens = slice((unit // SIDES) * GROUP_TOKENS, (unit // SIDES + 1) * GROUP_TOKENS)
+            for i in range(2):
+                j = (unit % SIDES) * HEADS + 2 * (s % 2) + i
+                w_cols = slice(j * P, (j + 1) * P)
+                acc[s, i] = bank_pool.tile([P, GROUP_TOKENS], F32, tag="bank", name="acc")
+                nc.tensor.matmul_mx(
+                    out=acc[s, i][:],
+                    lhsT=w_codes[:, w_cols].bitcast(FP8X4),
+                    lhsT_scale=w_scales[:, w_cols],
+                    rhs=h_codes[:, tokens].bitcast(FP8X4),
+                    rhs_scale=h_scales[:, tokens],
+                    start=True,
+                    stop=True,
+                )
+
+        def scale_and_square(s):
+            if s < 0 or s >= STEPS:
+                return
+            unit = s // 2
+            for i in range(2):
+                head = 2 * (s % 2) + i
+                j = (unit % SIDES) * HEADS + head
+                zt[unit, head] = zt_pool.tile([P, GROUP_TOKENS], F32, name="zt")
+                nc.scalar.activation(
+                    out=zt[unit, head][:],
+                    in_=acc[s, i][:],
+                    func=ACT.Identity,
+                    bias=gain_bias[:, j : j + 1],
+                    scale=gain_col[:, j : j + 1],
+                )
+                ysq[unit, head] = ysq_pool.tile([P, GROUP_TOKENS], F32, name="ysq")
+                nc.scalar.activation(
+                    out=ysq[unit, head][:],
+                    in_=acc[s, i][:],
+                    func=ACT.Square,
+                    bias=bias_col[:, j : j + 1],
+                )
+
+        def sum_squares(s):
+            if s < 0 or s >= STEPS:
+                return
+            unit = s // 2
+            if s % 2 == 0:
+                sq[unit] = ss_pool.tile([P, GROUP, HEAD], F32, name="sq")
+            for i in range(2):
+                t = 2 * (s % 2) + i
+                for head in range(HEADS):
+                    nc.tensor.matmul(
+                        out=sq[unit][:, t, :],
+                        lhsT=ysq[unit, head][:, t * P : (t + 1) * P],
+                        rhs=ident[:],
+                        is_transpose=True,
+                        start=(head == 0),
+                        stop=(head == HEADS - 1),
+                    )
+
+        def reduce_on_vector(unit):
+            if unit < 0 or unit >= UNITS or unit % 2 == 1:
+                return
+            ss[unit] = small.tile([P, GROUP], F32, name="ss")
+            nc.vector.tensor_reduce(
+                out=ss[unit][:], in_=sq[unit][:], axis=mybir.AxisListType.X, op=ALU.add
+            )
+
+        def reduce_on_scalar(unit):
+            if unit < 0 or unit >= UNITS or unit % 2 == 0:
+                return
+            ss[unit] = small.tile([P, GROUP], F32, name="ss")
+            junk = junk_pool.tile([P, GROUP, HEAD], F32)
+            for t in range(GROUP):
+                nc.scalar.activation(
+                    out=junk[:, t, :],
+                    in_=sq[unit][:, t, :],
+                    func=ACT.Identity,
+                    accum_out=ss[unit][:, t : t + 1],
+                )
+
+        def root(unit):
+            if unit < 0 or unit >= UNITS:
+                return
+            std[unit] = small.tile([P, GROUP], F32, name="std")
+            nc.scalar.activation(
+                out=std[unit][:], in_=ss[unit][:], func=ACT.Sqrt, bias=eps[:], scale=1.0 / DIM
+            )
+
+        def invert(unit):
+            if unit < 0 or unit >= UNITS:
+                return
+            rstd[unit] = small.tile([P, GROUP], F32, name="rstd")
+            nc.vector.reciprocal(out=rstd[unit][:], in_=std[unit][:])
+
+        def turn_back(s, i):
+            if s < 0 or s >= STEPS:
+                return
+            unit = s // 2
+            t = 2 * (s % 2) + i
+            z[s, i] = bank_pool.tile([P, HEADS, HEAD], F32, tag="bank", name="z")
+            for head in range(HEADS):
+                nc.tensor.transpose(
+                    z[s, i][:, head, :], zt[unit, head][:, t * P : (t + 1) * P], ident[:]
+                )
+
+        def rotate(s):
+            if s < 0 or s >= STEPS:
+                return
+            unit = s // 2
+            with_cos[s] = cos_pool.tile([P, 2, DIM], F32, name="with_cos")
+            with_sin[s] = sin_pool.tile([P, 2, DIM], F32, name="with_sin")
+            for i in range(2):
+                t = 2 * (s % 2) + i
+                T = (unit // SIDES) * GROUP + t
+                for table, product in ((cos_sb, with_cos[s]), (sin_swap, with_sin[s])):
+                    nc.vector.scalar_tensor_tensor(
+                        out=product[:, i, :].rearrange("p (h d) -> p h d", d=HEAD),
+                        in0=z[s, i][:],
+                        scalar=rstd[unit][:, t : t + 1],
+                        in1=table[:, T, :].unsqueeze(1).to_broadcast([P, HEADS, HEAD]),
+                        op0=ALU.mult,
+                        op1=ALU.mult,
+                    )
+
+        def combine_store(s):
+            if s < 0 or s >= STEPS:
+                return
+            engine = nc.vector if s == STEPS - 1 else nc.gpsimd
+            c_halves = with_cos[s][:].rearrange("p t (h x d) -> p (t h) x d", x=2, d=HALF)
+            s_halves = with_sin[s][:].rearrange("p t (h x d) -> p (t h) x d", x=2, d=HALF)
+            engine.tensor_tensor(
+                out=c_halves[:, :, 0, :],
+                in0=c_halves[:, :, 0, :],
+                in1=s_halves[:, :, 1, :],
+                op=ALU.subtract,
+            )
+            engine.tensor_tensor(
+                out=c_halves[:, :, 1, :],
+                in0=c_halves[:, :, 1, :],
+                in1=s_halves[:, :, 0, :],
+                op=ALU.add,
+            )
+            unit = s // 2
+            first = (unit // SIDES) * GROUP + 2 * (s % 2)
+            nc.sync.dma_start(
+                out=out_dram[unit % SIDES][:, first : first + 2, :], in_=with_cos[s][:]
+            )
+
+        for k in range(-1, STEPS + 6):
+            project(k + 1)
+            sum_squares(k - 2)
+            turn_back(k - 4, 0)
+            turn_back(k - 4, 1)
+            scale_and_square(k)
+            if k % 2 == 0:
+                reduce_on_scalar((k - 4) // 2)
+                root((k - 4) // 2)
+            rotate(k - 5)
+            if k % 2 == 1:
+                reduce_on_vector((k - 3) // 2)
+            if k % 2 == 0:
+                invert((k - 4) // 2)
+            if k + 2 < GROUPS:
+                turn_hidden(k + 2, False)
+            if 1 <= k + 1 < GROUPS:
+                quantise_hidden(k + 1)
+            combine_store(k - 6)

@@ -20,14 +20,18 @@ HEADS = DIM // HEAD
 SIDES = 2
 WORDS = DIM // 2
 TILES = TOKENS // P
-GROUP = 4
-GROUPS = TILES // GROUP
-GROUP_TOKENS = GROUP * P
-UNITS = GROUPS * SIDES
-STEPS = 2 * UNITS
+PAIRS = SIDES * HEADS // 2
 EPS = 1e-6
 
 FLOPS = 2 * TOKENS * SIDES * DIM * DIM
+
+GROUP_SIZES = [2, 4, 4, 4, 4, 4, 4, 4, 2]
+GROUP_FIRST = [sum(GROUP_SIZES[:g]) for g in range(len(GROUP_SIZES))]
+GROUPS = len(GROUP_SIZES)
+UNITS = GROUPS * SIDES
+
+STEPS = [(unit, half) for unit in range(UNITS) for half in range(GROUP_SIZES[unit // SIDES] // 2)]
+LAST_STEP = [max(s for s, step in enumerate(STEPS) if step[0] == unit) for unit in range(UNITS)]
 
 
 def turn_two_blocks(nc, bank, ident, two_blocks):
@@ -62,20 +66,19 @@ def tile_dynamicselfattention_pa_t_kernel(
         keep = stack.enter_context(tc.tile_pool(name="keep", bufs=1))
         quant = stack.enter_context(tc.tile_pool(name="quant", bufs=2))
         zt_pool = stack.enter_context(tc.tile_pool(name="zt_pool", bufs=16))
-        ysq_pool = stack.enter_context(tc.tile_pool(name="ysq_pool", bufs=12))
+        ysq_pool = stack.enter_context(tc.tile_pool(name="ysq_pool", bufs=10))
         small = stack.enter_context(tc.tile_pool(name="small", bufs=4))
-        cos_pool = stack.enter_context(tc.tile_pool(name="cos_pool", bufs=7))
-        sin_pool = stack.enter_context(tc.tile_pool(name="sin_pool", bufs=6))
         junk_pool = stack.enter_context(tc.tile_pool(name="junk_pool", bufs=2))
-        bank_pool = stack.enter_context(tc.psum_pool(name="bank_pool", bufs=6))
-        ss_pool = stack.enter_context(tc.psum_pool(name="ss_pool", bufs=2))
+        cos_pool = stack.enter_context(tc.tile_pool(name="cos_pool", bufs=6))
+        sin_pool = stack.enter_context(tc.tile_pool(name="sin_pool", bufs=5))
+        acc_pool = stack.enter_context(tc.psum_pool(name="acc_pool", bufs=3))
+        z_pool = stack.enter_context(tc.psum_pool(name="z_pool", bufs=4))
+        sq_pool = stack.enter_context(tc.psum_pool(name="sq_pool", bufs=1))
 
-        eps = keep.tile([P, 1], F32)
-        nc.vector.memset(eps[:], EPS)
-        warm = keep.tile([P, 1], F32)
-        nc.scalar.activation(out=warm[:], in_=eps[:], func=ACT.Sqrt)
         vec_rows = keep.tile([P, P], BF16)
         nc.vector.memset(vec_rows[:], 0.0)
+        eps = keep.tile([P, 1], F32)
+        nc.vector.memset(eps[:], EPS)
         ident = keep.tile([P, P], F32)
         make_identity(nc, ident[:])
 
@@ -83,31 +86,47 @@ def tile_dynamicselfattention_pa_t_kernel(
         w_rows = w_sb[:].rearrange("p (j k) -> p j k", k=DIM)
         h_sb = keep.tile([P, TILES * DIM], BF16)
         h_rows = h_sb[:].rearrange("p (T k) -> p T k", k=DIM)
+        cos_sb = keep.tile([P, TILES, HEAD], BF16)
+        sin_sb = keep.tile([P, TILES, HEAD], BF16)
+        sin_swap = keep.tile([P, TILES, HEAD], BF16)
 
         def load_w(pair):
             two = slice(2 * pair, 2 * pair + 2)
             nc.sync.dma_start(out=w_rows[:, two, :], in_=w_dram[:, two, :])
 
         def load_h(g):
-            four = slice(g * GROUP, (g + 1) * GROUP)
-            nc.sync.dma_start(out=h_rows[:, four, :], in_=h_dram[:, four, :])
+            some = slice(GROUP_FIRST[g], GROUP_FIRST[g] + GROUP_SIZES[g])
+            nc.sync.dma_start(out=h_rows[:, some, :], in_=h_dram[:, some, :])
 
-        nc.scalar.dma_start(out=vec_rows[0:8, :], in_=b_qk.rearrange("(j d) -> j d", d=HEAD))
-        nc.scalar.dma_start(out=vec_rows[8:12, :], in_=g_q.rearrange("(j d) -> j d", d=HEAD))
-        nc.scalar.dma_start(out=vec_rows[12:16, :], in_=g_k.rearrange("(j d) -> j d", d=HEAD))
-        load_w(0)
-        load_h(0)
-        for pair in range(1, SIDES * HEADS // 2):
-            load_w(pair)
-        cos_sb = keep.tile([P, TILES, HEAD], BF16)
-        sin_swap = keep.tile([P, TILES, HEAD], BF16)
-        for part in range(2):
-            for g in range(max(1, part * GROUPS // 2), (part + 1) * GROUPS // 2):
-                load_h(g)
-            some = slice(part * TILES // 2, (part + 1) * TILES // 2)
+        def load_tables(first, last):
+            some = slice(first, last)
+            nc.sync.dma_start(out=sin_sb[:, some, :], in_=sin_dram[:, some, :])
             nc.sync.dma_start(out=cos_sb[:, some, :], in_=cos_dram[:, some, :])
-            nc.sync.dma_start(out=sin_swap[:, some, 0:HALF], in_=sin_dram[:, some, HALF:HEAD])
-            nc.sync.dma_start(out=sin_swap[:, some, HALF:HEAD], in_=sin_dram[:, some, 0:HALF])
+            for x, sign in ((0, 1.0), (1, -1.0)):
+                nc.gpsimd.tensor_scalar(
+                    out=sin_swap[:, some, x * HALF : (x + 1) * HALF],
+                    in0=sin_sb[:, some, (1 - x) * HALF : (2 - x) * HALF],
+                    scalar1=sign,
+                    scalar2=0.0,
+                    op0=ALU.mult,
+                    op1=ALU.add,
+                )
+
+        load_w(0)
+        nc.sync.dma_start(out=vec_rows[0:8, :], in_=b_qk.rearrange("(j d) -> j d", d=HEAD))
+        nc.sync.dma_start(out=vec_rows[8:12, :], in_=g_q.rearrange("(j d) -> j d", d=HEAD))
+        nc.sync.dma_start(out=vec_rows[12:16, :], in_=g_k.rearrange("(j d) -> j d", d=HEAD))
+        load_h(0)
+        for pair in range(1, PAIRS):
+            load_w(pair)
+        load_h(1)
+        load_tables(0, 8)
+        load_h(2)
+        load_tables(8, TILES)
+        for g in range(3, GROUPS):
+            load_h(g)
+        warm = keep.tile([P, 1], F32)
+        nc.scalar.activation(out=warm[:], in_=eps[:], func=ACT.Sqrt)
 
         w_words = w_sb[:].bitcast(F32).rearrange("p (j w) -> p j w", w=WORDS)
         h_words = h_sb[:].bitcast(F32).rearrange("p (T w) -> p T w", w=WORDS)
@@ -120,7 +139,7 @@ def tile_dynamicselfattention_pa_t_kernel(
         h_grouped = {}
 
         def turn_weights(pair, on_scalar):
-            bank = bank_pool.tile([P, 2, 2, P], F32, tag="bank")
+            bank = z_pool.tile([P, 2, 2, P], F32, tag="z", name="w_turned")
             two = slice(2 * pair, 2 * pair + 2)
             turn_two_blocks(nc, bank, ident[:], w_words[:, two, :])
             copy_two_blocks(nc, bank, w_grouped_words[:, two], on_scalar)
@@ -132,42 +151,51 @@ def tile_dynamicselfattention_pa_t_kernel(
                 in_=w_grouped[:, 8 * P * pair : 8 * P * (pair + 1)],
             )
 
-        def turn_hidden(g, second_on_scalar):
-            h_grouped[g] = quant.tile([P, GROUP_TOKENS * 4], BF16, align_bytes=64, name="h_grouped")
+        h_turned = {}
+
+        def turn_hidden(g, pair):
+            first = GROUP_FIRST[g] + 2 * pair
+            h_turned[g, pair] = z_pool.tile([P, 2, 2, P], F32, tag="z", name="h_turned")
+            turn_two_blocks(nc, h_turned[g, pair], ident[:], h_words[:, first : first + 2, :])
+
+        def copy_hidden(g, pair, on_scalar):
+            if pair == 0:
+                h_grouped[g] = quant.tile([P, 16 * P], BF16, align_bytes=64, name="h_grouped")
             words = h_grouped[g][:].bitcast(F32).rearrange("p (t r u) -> p t r u", r=P, u=2)
-            for pair in range(GROUP // 2):
-                first = g * GROUP + 2 * pair
-                bank = bank_pool.tile([P, 2, 2, P], F32, tag="bank")
-                turn_two_blocks(nc, bank, ident[:], h_words[:, first : first + 2, :])
-                copy_two_blocks(
-                    nc, bank, words[:, 2 * pair : 2 * pair + 2], second_on_scalar and pair == 1
-                )
+            copy_two_blocks(nc, h_turned[g, pair], words[:, 2 * pair : 2 * pair + 2], on_scalar)
+
+        def group_tokens(g):
+            return slice(GROUP_FIRST[g] * P, (GROUP_FIRST[g] + GROUP_SIZES[g]) * P)
 
         def quantise_hidden(g):
-            tokens = slice(g * GROUP_TOKENS, (g + 1) * GROUP_TOKENS)
             nc.vector.quantize_mx(
-                out=h_codes[:, tokens].bitcast(FP8X4), scales=h_scales[:, tokens], in_=h_grouped[g][:]
+                out=h_codes[:, group_tokens(g)].bitcast(FP8X4),
+                scales=h_scales[:, group_tokens(g)],
+                in_=h_grouped[g][:, : 4 * P * GROUP_SIZES[g]],
             )
 
-        vec_f32 = keep.tile([P, P], F32)
-        nc.vector.tensor_copy(out=vec_f32[:], in_=vec_rows[:])
-        vec_ps = bank_pool.tile([P, P], F32, tag="bank")
-        nc.tensor.transpose(vec_ps[:], vec_f32[:], ident[:])
         cols = keep.tile([P, 16], F32)
-        nc.vector.tensor_copy(out=cols[:], in_=vec_ps[:, 0:16])
         bias_col = cols[:, 0:8]
         gain_col = cols[:, 8:16]
         gain_bias = keep.tile([P, 8], F32)
-        nc.vector.tensor_mul(out=gain_bias[:], in0=bias_col, in1=gain_col)
 
+        vec_f32 = keep.tile([P, P], F32)
+        nc.vector.tensor_copy(out=vec_f32[:], in_=vec_rows[:])
         turn_weights(0, False)
-        turn_hidden(0, True)
+        vec_ps = sq_pool.tile([P, P], F32, tag="sq", name="vec_ps")
+        nc.tensor.transpose(vec_ps[:], vec_f32[:], ident[:])
+        nc.vector.tensor_copy(out=cols[:], in_=vec_ps[:, 0:16])
+        turn_hidden(0, 0)
+        copy_hidden(0, 0, True)
         quantise_weights(0)
-        for pair in range(1, SIDES * HEADS // 2):
-            turn_weights(pair, True)
         quantise_hidden(0)
-        for pair in range(1, SIDES * HEADS // 2):
-            quantise_weights(pair)
+        turn_weights(1, True)
+        nc.vector.tensor_mul(out=gain_bias[:], in0=bias_col, in1=gain_col)
+        quantise_weights(1)
+        turn_weights(2, False)
+        turn_weights(3, False)
+        quantise_weights(2)
+        quantise_weights(3)
 
         acc = {}
         zt = {}
@@ -180,17 +208,26 @@ def tile_dynamicselfattention_pa_t_kernel(
         with_cos = {}
         with_sin = {}
 
+        def step_heads(s):
+            unit, half = STEPS[s]
+            size = GROUP_SIZES[unit // SIDES]
+            count = HEADS // (size // 2)
+            return [(half * count + i, i * size * P) for i in range(count)]
+
         def project(s):
-            if s < 0 or s >= STEPS:
+            if s < 0 or s >= len(STEPS):
                 return
-            unit = s // 2
-            tokens = slice((unit // SIDES) * GROUP_TOKENS, (unit // SIDES + 1) * GROUP_TOKENS)
-            for i in range(2):
-                j = (unit % SIDES) * HEADS + 2 * (s % 2) + i
+            unit = STEPS[s][0]
+            tokens = group_tokens(unit // SIDES)
+            width = GROUP_SIZES[unit // SIDES] * P
+            for head, at in step_heads(s):
+                if at % 512 == 0:
+                    bank = acc_pool.tile([P, 512], F32, tag="acc", name="acc_bank")
+                acc[unit, head] = bank[:, at % 512 : at % 512 + width]
+                j = (unit % SIDES) * HEADS + head
                 w_cols = slice(j * P, (j + 1) * P)
-                acc[s, i] = bank_pool.tile([P, GROUP_TOKENS], F32, tag="bank", name="acc")
                 nc.tensor.matmul_mx(
-                    out=acc[s, i][:],
+                    out=acc[unit, head],
                     lhsT=w_codes[:, w_cols].bitcast(FP8X4),
                     lhsT_scale=w_scales[:, w_cols],
                     rhs=h_codes[:, tokens].bitcast(FP8X4),
@@ -199,37 +236,35 @@ def tile_dynamicselfattention_pa_t_kernel(
                     stop=True,
                 )
 
-        def scale_and_square(s):
-            if s < 0 or s >= STEPS:
+        def scale_and_square(s, bank):
+            if s < 0 or s >= len(STEPS):
                 return
-            unit = s // 2
-            for i in range(2):
-                head = 2 * (s % 2) + i
+            unit = STEPS[s][0]
+            width = GROUP_SIZES[unit // SIDES] * P
+            for head, at in step_heads(s):
+                if at // 512 != bank:
+                    continue
                 j = (unit % SIDES) * HEADS + head
-                zt[unit, head] = zt_pool.tile([P, GROUP_TOKENS], F32, name="zt")
+                ysq[unit, head] = ysq_pool.tile([P, 512], F32, name="ysq")
                 nc.scalar.activation(
-                    out=zt[unit, head][:],
-                    in_=acc[s, i][:],
+                    out=ysq[unit, head][:, :width],
+                    in_=acc[unit, head],
+                    func=ACT.Square,
+                    bias=bias_col[:, j : j + 1],
+                )
+                zt[unit, head] = zt_pool.tile([P, 512], F32, name="zt")
+                nc.scalar.activation(
+                    out=zt[unit, head][:, :width],
+                    in_=acc[unit, head],
                     func=ACT.Identity,
                     bias=gain_bias[:, j : j + 1],
                     scale=gain_col[:, j : j + 1],
                 )
-                ysq[unit, head] = ysq_pool.tile([P, GROUP_TOKENS], F32, name="ysq")
-                nc.scalar.activation(
-                    out=ysq[unit, head][:],
-                    in_=acc[s, i][:],
-                    func=ACT.Square,
-                    bias=bias_col[:, j : j + 1],
-                )
 
-        def sum_squares(s):
-            if s < 0 or s >= STEPS:
-                return
-            unit = s // 2
-            if s % 2 == 0:
-                sq[unit] = ss_pool.tile([P, GROUP, HEAD], F32, name="sq")
-            for i in range(2):
-                t = 2 * (s % 2) + i
+        def sum_squares(unit):
+            size = GROUP_SIZES[unit // SIDES]
+            sq[unit] = sq_pool.tile([P, size, HEAD], F32, tag="sq", name="sq")
+            for t in range(size):
                 for head in range(HEADS):
                     nc.tensor.matmul(
                         out=sq[unit][:, t, :],
@@ -240,111 +275,120 @@ def tile_dynamicselfattention_pa_t_kernel(
                         stop=(head == HEADS - 1),
                     )
 
-        def reduce_on_vector(unit):
-            if unit < 0 or unit >= UNITS or unit % 2 == 1:
+        def reduce_squares(unit, on_scalar):
+            size = GROUP_SIZES[unit // SIDES]
+            ss[unit] = small.tile([P, 4], F32, name="ss")
+            if on_scalar:
+                junk = junk_pool.tile([P, 4, HEAD], F32)
+                for t in range(size):
+                    nc.scalar.activation(
+                        out=junk[:, t, :],
+                        in_=sq[unit][:, t, :],
+                        func=ACT.Identity,
+                        accum_out=ss[unit][:, t : t + 1],
+                    )
                 return
-            ss[unit] = small.tile([P, GROUP], F32, name="ss")
             nc.vector.tensor_reduce(
-                out=ss[unit][:], in_=sq[unit][:], axis=mybir.AxisListType.X, op=ALU.add
+                out=ss[unit][:, :size], in_=sq[unit][:], axis=mybir.AxisListType.X, op=ALU.add
             )
 
-        def reduce_on_scalar(unit):
-            if unit < 0 or unit >= UNITS or unit % 2 == 0:
-                return
-            ss[unit] = small.tile([P, GROUP], F32, name="ss")
-            junk = junk_pool.tile([P, GROUP, HEAD], F32)
-            for t in range(GROUP):
-                nc.scalar.activation(
-                    out=junk[:, t, :],
-                    in_=sq[unit][:, t, :],
-                    func=ACT.Identity,
-                    accum_out=ss[unit][:, t : t + 1],
-                )
-
         def root(unit):
-            if unit < 0 or unit >= UNITS:
-                return
-            std[unit] = small.tile([P, GROUP], F32, name="std")
+            size = GROUP_SIZES[unit // SIDES]
+            std[unit] = small.tile([P, 4], F32, name="std")
             nc.scalar.activation(
-                out=std[unit][:], in_=ss[unit][:], func=ACT.Sqrt, bias=eps[:], scale=1.0 / DIM
+                out=std[unit][:, :size],
+                in_=ss[unit][:, :size],
+                func=ACT.Sqrt,
+                bias=eps[:],
+                scale=1.0 / DIM,
             )
 
         def invert(unit):
-            if unit < 0 or unit >= UNITS:
-                return
-            rstd[unit] = small.tile([P, GROUP], F32, name="rstd")
-            nc.vector.reciprocal(out=rstd[unit][:], in_=std[unit][:])
+            size = GROUP_SIZES[unit // SIDES]
+            rstd[unit] = small.tile([P, 4], F32, name="rstd")
+            nc.vector.reciprocal(out=rstd[unit][:, :size], in_=std[unit][:, :size])
 
         def turn_back(s, i):
-            if s < 0 or s >= STEPS:
-                return
-            unit = s // 2
-            t = 2 * (s % 2) + i
-            z[s, i] = bank_pool.tile([P, HEADS, HEAD], F32, tag="bank", name="z")
+            unit, half = STEPS[s]
+            t = 2 * half + i
+            z[s, i] = z_pool.tile([P, HEADS, HEAD], F32, tag="z", name="z")
             for head in range(HEADS):
                 nc.tensor.transpose(
                     z[s, i][:, head, :], zt[unit, head][:, t * P : (t + 1) * P], ident[:]
                 )
 
-        def rotate(s):
-            if s < 0 or s >= STEPS:
-                return
-            unit = s // 2
-            with_cos[s] = cos_pool.tile([P, 2, DIM], F32, name="with_cos")
-            with_sin[s] = sin_pool.tile([P, 2, DIM], F32, name="with_sin")
-            for i in range(2):
-                t = 2 * (s % 2) + i
-                T = (unit // SIDES) * GROUP + t
-                for table, product in ((cos_sb, with_cos[s]), (sin_swap, with_sin[s])):
-                    nc.vector.scalar_tensor_tensor(
-                        out=product[:, i, :].rearrange("p (h d) -> p h d", d=HEAD),
-                        in0=z[s, i][:],
-                        scalar=rstd[unit][:, t : t + 1],
-                        in1=table[:, T, :].unsqueeze(1).to_broadcast([P, HEADS, HEAD]),
-                        op0=ALU.mult,
-                        op1=ALU.mult,
-                    )
+        def rotate(s, i):
+            unit, half = STEPS[s]
+            t = 2 * half + i
+            T = GROUP_FIRST[unit // SIDES] + t
+            if i == 0:
+                with_cos[s] = cos_pool.tile([P, 2, DIM], F32, name="with_cos")
+                with_sin[s] = sin_pool.tile([P, 2, DIM], F32, name="with_sin")
+            for table, product in ((cos_sb, with_cos[s]), (sin_swap, with_sin[s])):
+                nc.vector.scalar_tensor_tensor(
+                    out=product[:, i, :].rearrange("p (h d) -> p h d", d=HEAD),
+                    in0=z[s, i][:],
+                    scalar=rstd[unit][:, t : t + 1],
+                    in1=table[:, T, :].unsqueeze(1).to_broadcast([P, HEADS, HEAD]),
+                    op0=ALU.mult,
+                    op1=ALU.mult,
+                )
 
-        def combine_store(s):
-            if s < 0 or s >= STEPS:
-                return
-            engine = nc.vector if s == STEPS - 1 else nc.gpsimd
-            c_halves = with_cos[s][:].rearrange("p t (h x d) -> p (t h) x d", x=2, d=HALF)
-            s_halves = with_sin[s][:].rearrange("p t (h x d) -> p (t h) x d", x=2, d=HALF)
-            engine.tensor_tensor(
-                out=c_halves[:, :, 0, :],
-                in0=c_halves[:, :, 0, :],
-                in1=s_halves[:, :, 1, :],
-                op=ALU.subtract,
-            )
-            engine.tensor_tensor(
-                out=c_halves[:, :, 1, :],
-                in0=c_halves[:, :, 1, :],
-                in1=s_halves[:, :, 0, :],
-                op=ALU.add,
-            )
-            unit = s // 2
-            first = (unit // SIDES) * GROUP + 2 * (s % 2)
+        def add_and_store(s, engine, tiles):
+            unit, half = STEPS[s]
+            c_halves = with_cos[s][:, tiles].rearrange("p t (h x d) -> p (t h) x d", x=2, d=HALF)
+            s_halves = with_sin[s][:, tiles].rearrange("p t (h x d) -> p (t h) x d", x=2, d=HALF)
+            engine.tensor_tensor(out=c_halves, in0=c_halves, in1=s_halves[:, :, ::-1, :], op=ALU.add)
+            first = GROUP_FIRST[unit // SIDES] + 2 * half
             nc.sync.dma_start(
-                out=out_dram[unit % SIDES][:, first : first + 2, :], in_=with_cos[s][:]
+                out=out_dram[unit % SIDES][:, first + tiles.start : first + tiles.stop, :],
+                in_=with_cos[s][:, tiles],
             )
 
-        for k in range(-1, STEPS + 6):
+        rope_round = {}
+        for s, step in enumerate(STEPS):
+            rope_round[s] = LAST_STEP[step[0]] + 3 + step[1]
+        h_first = [min(s for s, step in enumerate(STEPS) if step[0] == SIDES * g) for g in range(GROUPS)]
+        pairs = [(g, pair) for g in range(1, GROUPS) for pair in range(GROUP_SIZES[g] // 2)]
+
+        for k in range(-1, len(STEPS) + 4):
+            roped = [s for s in range(len(STEPS)) if rope_round[s] == k]
+            roped_next = [s for s in range(len(STEPS)) if rope_round[s] == k + 1]
+            summed = [u for u in range(UNITS) if LAST_STEP[u] == k - 1]
+            rooted = [u for u in range(UNITS) if LAST_STEP[u] == k - 2]
+            turned = [(g, pair) for g, pair in pairs if (g - 2 if g < 3 else h_first[g] - 6 + pair) == k]
+            copied = [(g, pair) for g, pair in pairs if (g - 2 if g < 3 else h_first[g] - 5 + pair) == k]
+            quantised = [g for g in range(1, GROUPS) if (g - 2 if g < 3 else h_first[g] - 3) == k]
+
+            for u in rooted:
+                reduce_squares(u, u >= UNITS - 4)
+            for u in summed:
+                sum_squares(u)
+            for g, pair in turned:
+                turn_hidden(g, pair)
+                if (g, pair) in copied:
+                    copy_hidden(g, pair, False)
+            for g, pair in copied:
+                if (g, pair) not in turned:
+                    copy_hidden(g, pair, True)
             project(k + 1)
-            sum_squares(k - 2)
-            turn_back(k - 4, 0)
-            turn_back(k - 4, 1)
-            scale_and_square(k)
-            if k % 2 == 0:
-                reduce_on_scalar((k - 4) // 2)
-                root((k - 4) // 2)
-            rotate(k - 5)
-            if k % 2 == 1:
-                reduce_on_vector((k - 3) // 2)
-            if k % 2 == 0:
-                invert((k - 4) // 2)
-            if k + 2 < GROUPS:
-                turn_hidden(k + 2, False)
-            if 1 <= k + 1 < GROUPS:
-                quantise_hidden(k + 1)
-            combine_store(k - 6)
+            scale_and_square(k, 0)
+            for u in rooted:
+                root(u)
+            scale_and_square(k, 1)
+            for s in roped:
+                for i in range(2):
+                    rotate(s, i)
+            for s in roped_next:
+                for i in range(2):
+                    turn_back(s, i)
+            for u in rooted:
+                invert(u)
+            for g in quantised:
+                quantise_hidden(g)
+            for s in roped:
+                if s == len(STEPS) - 1:
+                    add_and_store(s, nc.gpsimd, slice(0, 1))
+                    add_and_store(s, nc.vector, slice(1, 2))
+                else:
+                    add_and_store(s, nc.gpsimd, slice(0, 2))

@@ -25,7 +25,7 @@ EPS = 1e-6
 
 FLOPS = 2 * TOKENS * SIDES * DIM * DIM
 
-GROUP_SIZES = [2, 4, 4, 4, 4, 4, 4, 4, 2]
+GROUP_SIZES = [2, 2, 4, 4, 4, 4, 4, 4, 4]
 GROUP_FIRST = [sum(GROUP_SIZES[:g]) for g in range(len(GROUP_SIZES))]
 GROUPS = len(GROUP_SIZES)
 UNITS = GROUPS * SIDES
@@ -69,11 +69,9 @@ def tile_dynamicselfattention_pa_t_kernel(
         ysq_pool = stack.enter_context(tc.tile_pool(name="ysq_pool", bufs=10))
         small = stack.enter_context(tc.tile_pool(name="small", bufs=4))
         junk_pool = stack.enter_context(tc.tile_pool(name="junk_pool", bufs=2))
-        cos_pool = stack.enter_context(tc.tile_pool(name="cos_pool", bufs=6))
-        sin_pool = stack.enter_context(tc.tile_pool(name="sin_pool", bufs=5))
-        acc_pool = stack.enter_context(tc.psum_pool(name="acc_pool", bufs=3))
+        roped_pool = stack.enter_context(tc.tile_pool(name="roped_pool", bufs=5))
+        acc_pool = stack.enter_context(tc.psum_pool(name="acc_pool", bufs=4))
         z_pool = stack.enter_context(tc.psum_pool(name="z_pool", bufs=4))
-        sq_pool = stack.enter_context(tc.psum_pool(name="sq_pool", bufs=1))
 
         vec_rows = keep.tile([P, P], BF16)
         nc.vector.memset(vec_rows[:], 0.0)
@@ -86,9 +84,8 @@ def tile_dynamicselfattention_pa_t_kernel(
         w_rows = w_sb[:].rearrange("p (j k) -> p j k", k=DIM)
         h_sb = keep.tile([P, TILES * DIM], BF16)
         h_rows = h_sb[:].rearrange("p (T k) -> p T k", k=DIM)
-        cos_sb = keep.tile([P, TILES, HEAD], BF16)
         sin_sb = keep.tile([P, TILES, HEAD], BF16)
-        sin_swap = keep.tile([P, TILES, HEAD], BF16)
+        tables = keep.tile([P, 2, TILES, HEAD], BF16)
 
         def load_w(pair):
             two = slice(2 * pair, 2 * pair + 2)
@@ -101,10 +98,10 @@ def tile_dynamicselfattention_pa_t_kernel(
         def load_tables(first, last):
             some = slice(first, last)
             nc.sync.dma_start(out=sin_sb[:, some, :], in_=sin_dram[:, some, :])
-            nc.sync.dma_start(out=cos_sb[:, some, :], in_=cos_dram[:, some, :])
+            nc.sync.dma_start(out=tables[:, 0, some, :], in_=cos_dram[:, some, :])
             for x, sign in ((0, 1.0), (1, -1.0)):
                 nc.gpsimd.tensor_scalar(
-                    out=sin_swap[:, some, x * HALF : (x + 1) * HALF],
+                    out=tables[:, 1, some, x * HALF : (x + 1) * HALF],
                     in0=sin_sb[:, some, (1 - x) * HALF : (2 - x) * HALF],
                     scalar1=sign,
                     scalar2=0.0,
@@ -126,7 +123,7 @@ def tile_dynamicselfattention_pa_t_kernel(
         for g in range(3, GROUPS):
             load_h(g)
         warm = keep.tile([P, 1], F32)
-        nc.scalar.activation(out=warm[:], in_=eps[:], func=ACT.Sqrt)
+        nc.scalar.activation(out=warm[:], in_=eps[:], func=ACT.Abs_reciprocal_sqrt)
 
         w_words = w_sb[:].bitcast(F32).rearrange("p (j w) -> p j w", w=WORDS)
         h_words = h_sb[:].bitcast(F32).rearrange("p (T w) -> p T w", w=WORDS)
@@ -182,7 +179,7 @@ def tile_dynamicselfattention_pa_t_kernel(
         vec_f32 = keep.tile([P, P], F32)
         nc.vector.tensor_copy(out=vec_f32[:], in_=vec_rows[:])
         turn_weights(0, False)
-        vec_ps = sq_pool.tile([P, P], F32, tag="sq", name="vec_ps")
+        vec_ps = z_pool.tile([P, P], F32, tag="z", name="vec_ps")
         nc.tensor.transpose(vec_ps[:], vec_f32[:], ident[:])
         nc.vector.tensor_copy(out=cols[:], in_=vec_ps[:, 0:16])
         turn_hidden(0, 0)
@@ -192,21 +189,15 @@ def tile_dynamicselfattention_pa_t_kernel(
         turn_weights(1, True)
         nc.vector.tensor_mul(out=gain_bias[:], in0=bias_col, in1=gain_col)
         quantise_weights(1)
-        turn_weights(2, False)
-        turn_weights(3, False)
-        quantise_weights(2)
-        quantise_weights(3)
 
         acc = {}
         zt = {}
         ysq = {}
         sq = {}
         ss = {}
-        std = {}
         rstd = {}
         z = {}
-        with_cos = {}
-        with_sin = {}
+        roped = {}
 
         def step_heads(s):
             unit, half = STEPS[s]
@@ -263,7 +254,7 @@ def tile_dynamicselfattention_pa_t_kernel(
 
         def sum_squares(unit):
             size = GROUP_SIZES[unit // SIDES]
-            sq[unit] = sq_pool.tile([P, size, HEAD], F32, tag="sq", name="sq")
+            sq[unit] = z_pool.tile([P, size, HEAD], F32, tag="z", name="sq")
             for t in range(size):
                 for head in range(HEADS):
                     nc.tensor.matmul(
@@ -292,21 +283,16 @@ def tile_dynamicselfattention_pa_t_kernel(
                 out=ss[unit][:, :size], in_=sq[unit][:], axis=mybir.AxisListType.X, op=ALU.add
             )
 
-        def root(unit):
+        def invert_root(unit):
             size = GROUP_SIZES[unit // SIDES]
-            std[unit] = small.tile([P, 4], F32, name="std")
+            rstd[unit] = small.tile([P, 4], F32, name="rstd")
             nc.scalar.activation(
-                out=std[unit][:, :size],
+                out=rstd[unit][:, :size],
                 in_=ss[unit][:, :size],
-                func=ACT.Sqrt,
+                func=ACT.Abs_reciprocal_sqrt,
                 bias=eps[:],
                 scale=1.0 / DIM,
             )
-
-        def invert(unit):
-            size = GROUP_SIZES[unit // SIDES]
-            rstd[unit] = small.tile([P, 4], F32, name="rstd")
-            nc.vector.reciprocal(out=rstd[unit][:, :size], in_=std[unit][:, :size])
 
         def turn_back(s, i):
             unit, half = STEPS[s]
@@ -322,27 +308,28 @@ def tile_dynamicselfattention_pa_t_kernel(
             t = 2 * half + i
             T = GROUP_FIRST[unit // SIDES] + t
             if i == 0:
-                with_cos[s] = cos_pool.tile([P, 2, DIM], F32, name="with_cos")
-                with_sin[s] = sin_pool.tile([P, 2, DIM], F32, name="with_sin")
-            for table, product in ((cos_sb, with_cos[s]), (sin_swap, with_sin[s])):
+                roped[s] = roped_pool.tile([P, 2, 2, DIM], F32, name="roped")
+            for part in range(2):
                 nc.vector.scalar_tensor_tensor(
-                    out=product[:, i, :].rearrange("p (h d) -> p h d", d=HEAD),
+                    out=roped[s][:, part, i].rearrange("p (h d) -> p h d", d=HEAD),
                     in0=z[s, i][:],
                     scalar=rstd[unit][:, t : t + 1],
-                    in1=table[:, T, :].unsqueeze(1).to_broadcast([P, HEADS, HEAD]),
+                    in1=tables[:, part, T, :].unsqueeze(1).to_broadcast([P, HEADS, HEAD]),
                     op0=ALU.mult,
                     op1=ALU.mult,
                 )
 
         def add_and_store(s, engine, tiles):
             unit, half = STEPS[s]
-            c_halves = with_cos[s][:, tiles].rearrange("p t (h x d) -> p (t h) x d", x=2, d=HALF)
-            s_halves = with_sin[s][:, tiles].rearrange("p t (h x d) -> p (t h) x d", x=2, d=HALF)
-            engine.tensor_tensor(out=c_halves, in0=c_halves, in1=s_halves[:, :, ::-1, :], op=ALU.add)
+            with_cos, with_sin = [
+                roped[s][:, part, tiles].rearrange("p t (h x d) -> p (t h) x d", x=2, d=HALF)
+                for part in range(2)
+            ]
+            engine.tensor_tensor(out=with_cos, in0=with_cos, in1=with_sin[:, :, ::-1, :], op=ALU.add)
             first = GROUP_FIRST[unit // SIDES] + 2 * half
             nc.sync.dma_start(
                 out=out_dram[unit % SIDES][:, first + tiles.start : first + tiles.stop, :],
-                in_=with_cos[s][:, tiles],
+                in_=roped[s][:, 0, tiles],
             )
 
         rope_round = {}
@@ -351,9 +338,14 @@ def tile_dynamicselfattention_pa_t_kernel(
         h_first = [min(s for s, step in enumerate(STEPS) if step[0] == SIDES * g) for g in range(GROUPS)]
         pairs = [(g, pair) for g in range(1, GROUPS) for pair in range(GROUP_SIZES[g] // 2)]
 
+        turn_weights(2, False)
+        project(0)
+        turn_weights(3, False)
+        quantise_weights(2)
+        quantise_weights(3)
         for k in range(-1, len(STEPS) + 4):
-            roped = [s for s in range(len(STEPS)) if rope_round[s] == k]
-            roped_next = [s for s in range(len(STEPS)) if rope_round[s] == k + 1]
+            in_rope = [s for s in range(len(STEPS)) if rope_round[s] == k]
+            next_in_rope = [s for s in range(len(STEPS)) if rope_round[s] == k + 1]
             summed = [u for u in range(UNITS) if LAST_STEP[u] == k - 1]
             rooted = [u for u in range(UNITS) if LAST_STEP[u] == k - 2]
             turned = [(g, pair) for g, pair in pairs if (g - 2 if g < 3 else h_first[g] - 6 + pair) == k]
@@ -371,23 +363,22 @@ def tile_dynamicselfattention_pa_t_kernel(
             for g, pair in copied:
                 if (g, pair) not in turned:
                     copy_hidden(g, pair, True)
-            project(k + 1)
+            if k >= 0:
+                project(k + 1)
             scale_and_square(k, 0)
             for u in rooted:
-                root(u)
+                invert_root(u)
             scale_and_square(k, 1)
-            for s in roped:
+            for s in in_rope:
                 for i in range(2):
                     rotate(s, i)
-            for s in roped_next:
+            for s in next_in_rope:
                 for i in range(2):
                     turn_back(s, i)
-            for u in rooted:
-                invert(u)
             for g in quantised:
                 quantise_hidden(g)
-            for s in roped:
-                if s == len(STEPS) - 1:
+            for s in in_rope:
+                if s >= len(STEPS) - 2:
                     add_and_store(s, nc.gpsimd, slice(0, 1))
                     add_and_store(s, nc.vector, slice(1, 2))
                 else:

@@ -25,7 +25,7 @@ EPS = 1e-6
 
 FLOPS = 2 * TOKENS * SIDES * DIM * DIM
 
-GROUP_SIZES = [2, 2, 4, 4, 4, 4, 4, 4, 4]
+GROUP_SIZES = [2, 4, 4, 4, 4, 4, 4, 4, 2]
 GROUP_FIRST = [sum(GROUP_SIZES[:g]) for g in range(len(GROUP_SIZES))]
 GROUPS = len(GROUP_SIZES)
 UNITS = GROUPS * SIDES
@@ -70,7 +70,8 @@ def tile_dynamicselfattention_pa_t_kernel(
         small = stack.enter_context(tc.tile_pool(name="small", bufs=4))
         junk_pool = stack.enter_context(tc.tile_pool(name="junk_pool", bufs=2))
         roped_pool = stack.enter_context(tc.tile_pool(name="roped_pool", bufs=5))
-        acc_pool = stack.enter_context(tc.psum_pool(name="acc_pool", bufs=4))
+        sq_pool = stack.enter_context(tc.psum_pool(name="sq_pool", bufs=1))
+        acc_pool = stack.enter_context(tc.psum_pool(name="acc_pool", bufs=3))
         z_pool = stack.enter_context(tc.psum_pool(name="z_pool", bufs=4))
 
         vec_rows = keep.tile([P, P], BF16)
@@ -179,7 +180,7 @@ def tile_dynamicselfattention_pa_t_kernel(
         vec_f32 = keep.tile([P, P], F32)
         nc.vector.tensor_copy(out=vec_f32[:], in_=vec_rows[:])
         turn_weights(0, False)
-        vec_ps = z_pool.tile([P, P], F32, tag="z", name="vec_ps")
+        vec_ps = sq_pool.tile([P, P], F32, tag="sq", name="vec_ps")
         nc.tensor.transpose(vec_ps[:], vec_f32[:], ident[:])
         nc.vector.tensor_copy(out=cols[:], in_=vec_ps[:, 0:16])
         turn_hidden(0, 0)
@@ -254,7 +255,7 @@ def tile_dynamicselfattention_pa_t_kernel(
 
         def sum_squares(unit):
             size = GROUP_SIZES[unit // SIDES]
-            sq[unit] = z_pool.tile([P, size, HEAD], F32, tag="z", name="sq")
+            sq[unit] = sq_pool.tile([P, size, HEAD], F32, tag="sq", name="sq")
             for t in range(size):
                 for head in range(HEADS):
                     nc.tensor.matmul(
@@ -378,8 +379,8 @@ def tile_dynamicselfattention_pa_t_kernel(
             for g in quantised:
                 quantise_hidden(g)
             for s in in_rope:
-                if s >= len(STEPS) - 2:
-                    add_and_store(s, nc.gpsimd, slice(0, 1))
+                if s == len(STEPS) - 1:
+                    add_and_store(s, nc.vector, slice(0, 1))
                     add_and_store(s, nc.vector, slice(1, 2))
                 else:
                     add_and_store(s, nc.gpsimd, slice(0, 2))

@@ -354,7 +354,7 @@ def tile_dynamicselfattention_pa_t_kernel(
             quantised = [g for g in range(1, GROUPS) if (g - 2 if g < 3 else h_first[g] - 3) == k]
 
             for u in rooted:
-                reduce_squares(u, u >= UNITS - 4)
+                reduce_squares(u, u >= UNITS - 2)
             for u in summed:
                 sum_squares(u)
             for g, pair in turned:

from contextlib import ExitStack

import concourse.mybir as mybir
from concourse.masks import make_identity

F32 = mybir.dt.float32
BF16 = mybir.dt.bfloat16
U32 = mybir.dt.uint32
U8 = mybir.dt.uint8
FP8X4 = mybir.dt.float8_e4m3fn_x4
ACT = mybir.ActivationFunctionType
ALU = mybir.AluOpType

P = 128
TOKENS = 4096
DIM = 512
HEAD = 128
HALF = HEAD // 2
HEADS = DIM // HEAD
SIDES = 2
WORDS = DIM // 2
TILES = TOKENS // P
PAIRS = SIDES * HEADS // 2
EPS = 1e-6

FLOPS = 2 * TOKENS * SIDES * DIM * DIM

GROUP_SIZES = [2, 4, 4, 4, 4, 4, 4, 4, 2]
GROUP_FIRST = [sum(GROUP_SIZES[:g]) for g in range(len(GROUP_SIZES))]
GROUPS = len(GROUP_SIZES)
UNITS = GROUPS * SIDES

STEPS = [(unit, half) for unit in range(UNITS) for half in range(GROUP_SIZES[unit // SIDES] // 2)]
LAST_STEP = [max(s for s, step in enumerate(STEPS) if step[0] == unit) for unit in range(UNITS)]


def turn_two_blocks(nc, bank, ident, two_blocks):
    for blk in range(2):
        for u in range(2):
            nc.tensor.transpose(bank[:, blk, u, :], two_blocks[:, blk, u:WORDS:2], ident)


def copy_two_blocks(nc, bank, grouped, on_scalar):
    planes = bank[:].rearrange("p b u r -> p b r u")
    if on_scalar:
        nc.scalar.copy(out=grouped, in_=planes)
    else:
        nc.vector.tensor_copy(out=grouped, in_=planes)


def tile_dynamicselfattention_pa_t_kernel(
    tc, hidden_states, cos, sin, w_qk, b_qk, g_q, g_k, out_0, out_1
):
    nc = tc.nc
    h_dram = hidden_states.flatten_outer_dims().rearrange("(p T) k -> p T k", T=TILES)
    cos_dram = cos.rearrange("(p T) d -> p T d", T=TILES)
    sin_dram = sin.rearrange("(p T) d -> p T d", T=TILES)
    w_dram = w_qk.rearrange("(j p) k -> p j k", p=P)
    out_dram = [
        o.flatten_outer_dims().rearrange("(p T h) d -> p T (h d)", T=TILES, h=HEADS)
        for o in (out_0, out_1)
    ]

    with ExitStack() as stack:
        stack.enter_context(tc.manual_schedule())
        keep = stack.enter_context(tc.tile_pool(name="keep", bufs=1))
        quant = stack.enter_context(tc.tile_pool(name="quant", bufs=2))
        zt_pool = stack.enter_context(tc.tile_pool(name="zt_pool", bufs=16))
        ysq_pool = stack.enter_context(tc.tile_pool(name="ysq_pool", bufs=10))
        small = stack.enter_context(tc.tile_pool(name="small", bufs=4))
        junk_pool = stack.enter_context(tc.tile_pool(name="junk_pool", bufs=2))
        roped_pool = stack.enter_context(tc.tile_pool(name="roped_pool", bufs=5))
        sq_pool = stack.enter_context(tc.psum_pool(name="sq_pool", bufs=1))
        acc_pool = stack.enter_context(tc.psum_pool(name="acc_pool", bufs=3))
        z_pool = stack.enter_context(tc.psum_pool(name="z_pool", bufs=4))

        vec_rows = keep.tile([P, P], BF16)
        nc.vector.memset(vec_rows[:], 0.0)
        eps = keep.tile([P, 1], F32)
        nc.vector.memset(eps[:], EPS)
        ident = keep.tile([P, P], F32)
        make_identity(nc, ident[:])

        w_sb = keep.tile([P, SIDES * HEADS * DIM], BF16)
        w_rows = w_sb[:].rearrange("p (j k) -> p j k", k=DIM)
        h_sb = keep.tile([P, TILES * DIM], BF16)
        h_rows = h_sb[:].rearrange("p (T k) -> p T k", k=DIM)
        sin_sb = keep.tile([P, TILES, HEAD], BF16)
        tables = keep.tile([P, 2, TILES, HEAD], BF16)

        def load_w(pair):
            two = slice(2 * pair, 2 * pair + 2)
            nc.sync.dma_start(out=w_rows[:, two, :], in_=w_dram[:, two, :])

        def load_h(g):
            some = slice(GROUP_FIRST[g], GROUP_FIRST[g] + GROUP_SIZES[g])
            nc.sync.dma_start(out=h_rows[:, some, :], in_=h_dram[:, some, :])

        def load_tables(first, last):
            some = slice(first, last)
            nc.sync.dma_start(out=sin_sb[:, some, :], in_=sin_dram[:, some, :])
            nc.sync.dma_start(out=tables[:, 0, some, :], in_=cos_dram[:, some, :])
            for x, sign in ((0, 1.0), (1, -1.0)):
                nc.gpsimd.tensor_scalar(
                    out=tables[:, 1, some, x * HALF : (x + 1) * HALF],
                    in0=sin_sb[:, some, (1 - x) * HALF : (2 - x) * HALF],
                    scalar1=sign,
                    scalar2=0.0,
                    op0=ALU.mult,
                    op1=ALU.add,
                )

        load_w(0)
        nc.sync.dma_start(out=vec_rows[0:8, :], in_=b_qk.rearrange("(j d) -> j d", d=HEAD))
        nc.sync.dma_start(out=vec_rows[8:12, :], in_=g_q.rearrange("(j d) -> j d", d=HEAD))
        nc.sync.dma_start(out=vec_rows[12:16, :], in_=g_k.rearrange("(j d) -> j d", d=HEAD))
        load_h(0)
        for pair in range(1, PAIRS):
            load_w(pair)
        load_h(1)
        load_tables(0, 8)
        load_h(2)
        load_tables(8, TILES)
        for g in range(3, GROUPS):
            load_h(g)
        warm = keep.tile([P, 1], F32)
        nc.scalar.activation(out=warm[:], in_=eps[:], func=ACT.Abs_reciprocal_sqrt)

        w_words = w_sb[:].bitcast(F32).rearrange("p (j w) -> p j w", w=WORDS)
        h_words = h_sb[:].bitcast(F32).rearrange("p (T w) -> p T w", w=WORDS)
        w_grouped = keep.tile([P, SIDES * DIM * 4], BF16, align_bytes=64)
        w_grouped_words = w_grouped[:].bitcast(F32).rearrange("p (j r u) -> p j r u", r=P, u=2)
        w_codes = keep.tile([P, SIDES * DIM], U32, align_bytes=64)
        w_scales = keep.tile([P, SIDES * DIM], U8, align_bytes=64)
        h_codes = keep.tile([P, TOKENS], U32, align_bytes=64)
        h_scales = keep.tile([P, TOKENS], U8, align_bytes=64)
        h_grouped = {}

        def turn_weights(pair, on_scalar):
            bank = z_pool.tile([P, 2, 2, P], F32, tag="z", name="w_turned")
            two = slice(2 * pair, 2 * pair + 2)
            turn_two_blocks(nc, bank, ident[:], w_words[:, two, :])
            copy_two_blocks(nc, bank, w_grouped_words[:, two], on_scalar)

        def quantise_weights(pair):
            nc.vector.quantize_mx(
                out=w_codes[:, 2 * P * pair : 2 * P * (pair + 1)].bitcast(FP8X4),
                scales=w_scales[:, 2 * P * pair : 2 * P * (pair + 1)],
                in_=w_grouped[:, 8 * P * pair : 8 * P * (pair + 1)],
            )

        h_turned = {}

        def turn_hidden(g, pair):
            first = GROUP_FIRST[g] + 2 * pair
            h_turned[g, pair] = z_pool.tile([P, 2, 2, P], F32, tag="z", name="h_turned")
            turn_two_blocks(nc, h_turned[g, pair], ident[:], h_words[:, first : first + 2, :])

        def copy_hidden(g, pair, on_scalar):
            if pair == 0:
                h_grouped[g] = quant.tile([P, 16 * P], BF16, align_bytes=64, name="h_grouped")
            words = h_grouped[g][:].bitcast(F32).rearrange("p (t r u) -> p t r u", r=P, u=2)
            copy_two_blocks(nc, h_turned[g, pair], words[:, 2 * pair : 2 * pair + 2], on_scalar)

        def group_tokens(g):
            return slice(GROUP_FIRST[g] * P, (GROUP_FIRST[g] + GROUP_SIZES[g]) * P)

        def quantise_hidden(g):
            nc.vector.quantize_mx(
                out=h_codes[:, group_tokens(g)].bitcast(FP8X4),
                scales=h_scales[:, group_tokens(g)],
                in_=h_grouped[g][:, : 4 * P * GROUP_SIZES[g]],
            )

        cols = keep.tile([P, 16], F32)
        bias_col = cols[:, 0:8]
        gain_col = cols[:, 8:16]
        gain_bias = keep.tile([P, 8], F32)

        vec_f32 = keep.tile([P, P], F32)
        nc.vector.tensor_copy(out=vec_f32[:], in_=vec_rows[:])
        turn_weights(0, False)
        vec_ps = sq_pool.tile([P, P], F32, tag="sq", name="vec_ps")
        nc.tensor.transpose(vec_ps[:], vec_f32[:], ident[:])
        nc.vector.tensor_copy(out=cols[:], in_=vec_ps[:, 0:16])
        turn_hidden(0, 0)
        copy_hidden(0, 0, True)
        quantise_weights(0)
        quantise_hidden(0)
        turn_weights(1, True)
        nc.vector.tensor_mul(out=gain_bias[:], in0=bias_col, in1=gain_col)
        quantise_weights(1)

        acc = {}
        zt = {}
        ysq = {}
        sq = {}
        ss = {}
        rstd = {}
        z = {}
        roped = {}

        def step_heads(s):
            unit, half = STEPS[s]
            size = GROUP_SIZES[unit // SIDES]
            count = HEADS // (size // 2)
            return [(half * count + i, i * size * P) for i in range(count)]

        def project(s):
            if s < 0 or s >= len(STEPS):
                return
            unit = STEPS[s][0]
            tokens = group_tokens(unit // SIDES)
            width = GROUP_SIZES[unit // SIDES] * P
            for head, at in step_heads(s):
                if at % 512 == 0:
                    bank = acc_pool.tile([P, 512], F32, tag="acc", name="acc_bank")
                acc[unit, head] = bank[:, at % 512 : at % 512 + width]
                j = (unit % SIDES) * HEADS + head
                w_cols = slice(j * P, (j + 1) * P)
                nc.tensor.matmul_mx(
                    out=acc[unit, head],
                    lhsT=w_codes[:, w_cols].bitcast(FP8X4),
                    lhsT_scale=w_scales[:, w_cols],
                    rhs=h_codes[:, tokens].bitcast(FP8X4),
                    rhs_scale=h_scales[:, tokens],
                    start=True,
                    stop=True,
                )

        def scale_and_square(s, bank):
            if s < 0 or s >= len(STEPS):
                return
            unit = STEPS[s][0]
            width = GROUP_SIZES[unit // SIDES] * P
            for head, at in step_heads(s):
                if at // 512 != bank:
                    continue
                j = (unit % SIDES) * HEADS + head
                ysq[unit, head] = ysq_pool.tile([P, 512], F32, name="ysq")
                nc.scalar.activation(
                    out=ysq[unit, head][:, :width],
                    in_=acc[unit, head],
                    func=ACT.Square,
                    bias=bias_col[:, j : j + 1],
                )
                zt[unit, head] = zt_pool.tile([P, 512], F32, name="zt")
                nc.scalar.activation(
                    out=zt[unit, head][:, :width],
                    in_=acc[unit, head],
                    func=ACT.Identity,
                    bias=gain_bias[:, j : j + 1],
                    scale=gain_col[:, j : j + 1],
                )

        def sum_squares(unit):
            size = GROUP_SIZES[unit // SIDES]
            sq[unit] = sq_pool.tile([P, size, HEAD], F32, tag="sq", name="sq")
            for t in range(size):
                for head in range(HEADS):
                    nc.tensor.matmul(
                        out=sq[unit][:, t, :],
                        lhsT=ysq[unit, head][:, t * P : (t + 1) * P],
                        rhs=ident[:],
                        is_transpose=True,
                        start=(head == 0),
                        stop=(head == HEADS - 1),
                    )

        def reduce_squares(unit, on_scalar):
            size = GROUP_SIZES[unit // SIDES]
            ss[unit] = small.tile([P, 4], F32, name="ss")
            if on_scalar:
                junk = junk_pool.tile([P, 4, HEAD], F32)
                for t in range(size):
                    nc.scalar.activation(
                        out=junk[:, t, :],
                        in_=sq[unit][:, t, :],
                        func=ACT.Identity,
                        accum_out=ss[unit][:, t : t + 1],
                    )
                return
            nc.vector.tensor_reduce(
                out=ss[unit][:, :size], in_=sq[unit][:], axis=mybir.AxisListType.X, op=ALU.add
            )

        def invert_root(unit):
            size = GROUP_SIZES[unit // SIDES]
            rstd[unit] = small.tile([P, 4], F32, name="rstd")
            nc.scalar.activation(
                out=rstd[unit][:, :size],
                in_=ss[unit][:, :size],
                func=ACT.Abs_reciprocal_sqrt,
                bias=eps[:],
                scale=1.0 / DIM,
            )

        def turn_back(s, i):
            unit, half = STEPS[s]
            t = 2 * half + i
            z[s, i] = z_pool.tile([P, HEADS, HEAD], F32, tag="z", name="z")
            for head in range(HEADS):
                nc.tensor.transpose(
                    z[s, i][:, head, :], zt[unit, head][:, t * P : (t + 1) * P], ident[:]
                )

        def rotate(s, i):
            unit, half = STEPS[s]
            t = 2 * half + i
            T = GROUP_FIRST[unit // SIDES] + t
            if i == 0:
                roped[s] = roped_pool.tile([P, 2, 2, DIM], F32, name="roped")
            for part in range(2):
                nc.vector.scalar_tensor_tensor(
                    out=roped[s][:, part, i].rearrange("p (h d) -> p h d", d=HEAD),
                    in0=z[s, i][:],
                    scalar=rstd[unit][:, t : t + 1],
                    in1=tables[:, part, T, :].unsqueeze(1).to_broadcast([P, HEADS, HEAD]),
                    op0=ALU.mult,
                    op1=ALU.mult,
                )

        def add_and_store(s, engine, tiles):
            unit, half = STEPS[s]
            with_cos, with_sin = [
                roped[s][:, part, tiles].rearrange("p t (h x d) -> p (t h) x d", x=2, d=HALF)
                for part in range(2)
            ]
            engine.tensor_tensor(out=with_cos, in0=with_cos, in1=with_sin[:, :, ::-1, :], op=ALU.add)
            first = GROUP_FIRST[unit // SIDES] + 2 * half
            nc.sync.dma_start(
                out=out_dram[unit % SIDES][:, first + tiles.start : first + tiles.stop, :],
                in_=roped[s][:, 0, tiles],
            )

        rope_round = {}
        for s, step in enumerate(STEPS):
            rope_round[s] = LAST_STEP[step[0]] + 3 + step[1]
        h_first = [min(s for s, step in enumerate(STEPS) if step[0] == SIDES * g) for g in range(GROUPS)]
        pairs = [(g, pair) for g in range(1, GROUPS) for pair in range(GROUP_SIZES[g] // 2)]

        turn_weights(2, False)
        project(0)
        turn_weights(3, False)
        quantise_weights(2)
        quantise_weights(3)
        for k in range(-1, len(STEPS) + 4):
            in_rope = [s for s in range(len(STEPS)) if rope_round[s] == k]
            next_in_rope = [s for s in range(len(STEPS)) if rope_round[s] == k + 1]
            summed = [u for u in range(UNITS) if LAST_STEP[u] == k - 1]
            rooted = [u for u in range(UNITS) if LAST_STEP[u] == k - 2]
            turned = [(g, pair) for g, pair in pairs if (g - 2 if g < 3 else h_first[g] - 6 + pair) == k]
            copied = [(g, pair) for g, pair in pairs if (g - 2 if g < 3 else h_first[g] - 5 + pair) == k]
            quantised = [g for g in range(1, GROUPS) if (g - 2 if g < 3 else h_first[g] - 3) == k]

            for u in rooted:
                reduce_squares(u, u >= UNITS - 2)
            for u in summed:
                sum_squares(u)
            for g, pair in turned:
                turn_hidden(g, pair)
                if (g, pair) in copied:
                    copy_hidden(g, pair, False)
            for g, pair in copied:
                if (g, pair) not in turned:
                    copy_hidden(g, pair, True)
            if k >= 0:
                project(k + 1)
            scale_and_square(k, 0)
            for u in rooted:
                invert_root(u)
            scale_and_square(k, 1)
            for s in in_rope:
                for i in range(2):
                    rotate(s, i)
            for s in next_in_rope:
                for i in range(2):
                    turn_back(s, i)
            for g in quantised:
                quantise_hidden(g)
            for s in in_rope:
                if s == len(STEPS) - 1:
                    add_and_store(s, nc.vector, slice(0, 1))
                    add_and_store(s, nc.vector, slice(1, 2))
                else:
                    add_and_store(s, nc.gpsimd, slice(0, 2))
